import numpy as np
import ml_dtypes


def mxq(x, axis, fmt="e4m3"):
    dtype, down = {"e4m3": (ml_dtypes.float8_e4m3fn, 7), "e5m2": (ml_dtypes.float8_e5m2, 14)}[fmt]
    v = np.moveaxis(np.asarray(x, np.float32).astype(ml_dtypes.bfloat16).astype(np.float64), axis, -1)
    blocks = v.reshape(v.shape[:-1] + (-1, 32))
    amax = np.abs(blocks).max(-1, keepdims=True)
    byte = np.maximum(np.where(amax > 0, np.frexp(amax)[1] - 1 + 127, 0) - down, 1)
    scale = np.exp2(byte - 127.0)
    codes = (blocks / scale).astype(np.float32).astype(dtype).astype(np.float64)
    return np.moveaxis((codes * scale).reshape(v.shape), -1, axis)


WIDE = False


def mx_kscale(k):
    if not WIDE:
        return np.ones(k)
    levels = np.array([10, -10, 5, -5, 0])
    a = np.random.permutation(np.resize(levels, k // 512 * 4)).reshape(k // 512, 4)
    idx = np.arange(k)
    return np.exp2(a[idx // 512, idx % 128 // 32])


BF16 = ml_dtypes.bfloat16


def bf(x):
    return np.asarray(x, np.float32).astype(BF16)


def f64(x):
    return np.asarray(x).astype(np.float64)


E2M1 = np.array([0.0, 0.5, 1.0, 1.5, 2.0, 3.0, 4.0, 6.0, -0.0, -0.5, -1.0, -1.5, -2.0, -3.0, -4.0, -6.0])


def pack_weight(w, fmt):
    k, n = w.shape
    w = f64(bf(w)).reshape(k // 32, 32, n)
    amax = np.abs(w).max(1)
    if fmt == "e4m3":
        byte = np.frexp(amax)[1] - 1 + 127 - 7
    else:
        mant, ex = np.frexp(amax / 6.0)
        byte = np.where(mant > 0.5, ex, ex - 1) + 127
    byte = np.clip(np.where(amax > 0, byte, 1), 1, 254)
    scaled = (w * np.exp2(127.0 - byte)[:, None, :]).reshape(k, n).astype(np.float32)
    by_word = np.ascontiguousarray(scaled.reshape(k // 512, 128, 4, n).transpose(0, 1, 3, 2))
    if fmt == "e4m3":
        words = by_word.astype(ml_dtypes.float8_e4m3fn).view(np.uint8)
    else:
        c = by_word.astype(ml_dtypes.float4_e2m1fn).view(np.uint8) & 0xF
        words = c[..., 0::2] | (c[..., 1::2] << 4)
    return np.ascontiguousarray(words), np.ascontiguousarray(byte.astype(np.uint8).reshape(k // 512, 16, n))


def unpack_weight(words, scales, fmt):
    g, p, n, _ = words.shape
    if fmt == "e4m3":
        vals = np.ascontiguousarray(words).view(ml_dtypes.float8_e4m3fn).astype(np.float64)
    else:
        nib = np.empty((g, p, n, 4), np.uint8)
        nib[..., 0::2] = words & 0xF
        nib[..., 1::2] = words >> 4
        vals = E2M1[nib]
    vals = vals * np.repeat(np.exp2(scales.astype(np.float64) - 127.0), 8, axis=1)[..., None]
    return vals.transpose(0, 1, 3, 2).reshape(g * 512, n)


BATCH, SEQ, IN_DIM, MID_DIM, OUT_DIM = 1, 128, 4096, 2048, 4096
CB = 2.0 ** -np.round(np.log2(IN_DIM) / 2)
CA = 2.0 ** -np.round(np.log2(MID_DIM) / 2)
FMT = "e4m3"


def signs(shape):
    return np.where(np.random.standard_normal(shape) >= 0, 1.0, -1.0)


def setup_inputs():
    s, t = mx_kscale(IN_DIM), mx_kscale(MID_DIM)
    x = bf(np.random.standard_normal((BATCH, SEQ, IN_DIM)) * s)
    scaling0 = bf(0.5 + np.random.uniform(size=IN_DIM))
    B_words, B_scales = pack_weight((signs((MID_DIM, IN_DIM)) * CB / s[None, :]).T, FMT)
    scaling2 = bf((0.5 + np.random.uniform(size=MID_DIM)) * t)
    A_words, A_scales = pack_weight((signs((OUT_DIM, MID_DIM)) * CA / t[None, :]).T, FMT)
    scaling4 = bf(0.5 + np.random.uniform(size=OUT_DIM))
    bias = bf(np.random.standard_normal(OUT_DIM))
    return {"x": x,
            "scaling0": scaling0,
            "B_words": B_words,
            "B_scales": B_scales,
            "scaling2": scaling2,
            "A_words": A_words,
            "A_scales": A_scales,
            "scaling4": scaling4,
            "bias": bias}


def reference(x, scaling0, B_words, B_scales, scaling2, A_words, A_scales, scaling4, bias):
    h = f64(x) * f64(scaling0)
    h = mxq(h, 2, "e4m3") @ unpack_weight(B_words, B_scales, FMT)
    h = h * f64(scaling2)
    h = mxq(h, 2, "e4m3") @ unpack_weight(A_words, A_scales, FMT)
    return h * f64(scaling4) + f64(bias)

@@ -1,0 +1,184 @@
+from contextlib import ExitStack
+
+import concourse.mybir as mybir
+from concourse.masks import make_identity
+
+F32 = mybir.dt.float32
+BF16 = mybir.dt.bfloat16
+I32 = mybir.dt.int32
+U8 = mybir.dt.uint8
+FP8X4 = mybir.dt.float8_e4m3fn_x4
+MULT = mybir.AluOpType.mult
+ADD = mybir.AluOpType.add
+
+P = 128
+IN_DIM, MID_DIM, OUT_DIM = 4096, 2048, 4096
+GB = IN_DIM // 512
+GA = MID_DIM // 512
+FLOPS = 2 * P * IN_DIM * MID_DIM + 2 * P * MID_DIM * OUT_DIM
+
+A_CHUNKS = [1024, 1024, 1024, 512, 256, 256]
+
+
+def tile_doublebinarylinear_w_kernel(
+    tc, x, scaling0, B_words, B_scales, scaling2, A_words, A_scales, scaling4, bias, out
+):
+    nc = tc.nc
+    xf = x.flatten_outer_dims()
+    of = out.flatten_outer_dims()
+    with ExitStack() as ctx:
+        keep = ctx.enter_context(tc.tile_pool(name="keep", bufs=1))
+        work = ctx.enter_context(tc.tile_pool(name="work", bufs=3))
+        ps_acc = ctx.enter_context(tc.psum_pool(name="ps_acc", bufs=4))
+        ps_tr = ctx.enter_context(tc.psum_pool(name="ps_tr", bufs=4))
+
+        x_sb = keep.tile([P, IN_DIM], BF16, align_bytes=64)
+        vecs = keep.tile([P, 512], BF16, align_bytes=64)
+        b_pl = keep.tile([P, 2, MID_DIM], U8, align_bytes=64)
+        a_pl = keep.tile([P, OUT_DIM], U8, align_bytes=64)
+        b_w = keep.tile([P, GB, MID_DIM], I32, align_bytes=64)
+        a_w = keep.tile([P, GA, OUT_DIM], I32, align_bytes=64)
+        ident_f = keep.tile([P, P], F32)
+        ident_b = keep.tile([P, P], BF16)
+        s_t = keep.tile([P, 12, 2], F32)
+        x_grp = keep.tile([P, GB, P, 4], BF16, align_bytes=64)
+        x_codes = keep.tile([P, GB * P], I32, align_bytes=64)
+        x_pl = keep.tile([P, GB * P], U8, align_bytes=64)
+        s4_b = keep.tile([P, OUT_DIM], BF16)
+        bias_b = keep.tile([P, OUT_DIM], BF16)
+        h1_sb = keep.tile([P, GA, 4, P], F32)
+        h_grp = keep.tile([P, GA, P, 4], BF16, align_bytes=64)
+        h_codes = keep.tile([P, GA * P], I32, align_bytes=64)
+        h_pl = keep.tile([P, GA * P], U8, align_bytes=64)
+        o_sb = keep.tile([P, OUT_DIM], F32)
+
+        nc.vector.memset(vecs[:], 0.0)
+        nc.vector.memset(b_pl[:].bitcast(I32), 0)
+        nc.vector.memset(a_pl[:].bitcast(I32), 0)
+        make_identity(nc, ident_f[:])
+        make_identity(nc, ident_b[:])
+
+        for h in range(2):
+            nc.sync.dma_start(out=x_sb[:, 2048 * h : 2048 * (h + 1)], in_=xf[:, 2048 * h : 2048 * (h + 1)])
+        nc.scalar.dma_start(out=vecs[0:8, :], in_=scaling0.rearrange("(g n) -> g n", n=512))
+        nc.scalar.dma_start(out=vecs[8:12, :], in_=scaling2.rearrange("(g n) -> g n", n=512))
+        nc.scalar.dma_start(out=vecs[12:20, :], in_=scaling4.rearrange("(g n) -> g n", n=512))
+        nc.scalar.dma_start(out=vecs[20:28, :], in_=bias.rearrange("(g n) -> g n", n=512))
+        for s in range(2):
+            for q in (0, 2, 1, 3):
+                nc.sync.dma_start(
+                    out=b_pl[32 * q : 32 * q + 16, s, :].bitcast(I32),
+                    in_=B_scales[4 * s : 4 * s + 4, 4 * q : 4 * q + 4, :].bitcast(I32),
+                )
+        for q in (0, 2, 1, 3):
+            nc.sync.dma_start(
+                out=a_pl[32 * q : 32 * q + 16, :].bitcast(I32),
+                in_=A_scales[:, 4 * q : 4 * q + 4, :].bitcast(I32),
+            )
+        for g in range(GB):
+            nc.sync.dma_start(out=b_w[:, g, :], in_=B_words[g].rearrange("p n t -> p (n t)").bitcast(I32))
+        c0 = 0
+        for w in A_CHUNKS:
+            nc.sync.dma_start(
+                out=a_w[:, :, c0 : c0 + w],
+                in_=A_words[:, :, c0 : c0 + w, :].rearrange("g p n t -> p g (n t)").bitcast(I32),
+            )
+            c0 += w
+
+        vw = vecs[:].bitcast(F32)
+        vt = ps_tr.tile([P, 2, P], F32, tag="tr")
+        for u in range(2):
+            nc.tensor.transpose(out=vt[:, u, :], in_=vw[:, u:256:2], identity=ident_f[:])
+        nc.vector.tensor_copy(out=s_t[:], in_=vt[:, :, 0:12].rearrange("p u w -> p w u"))
+        s_tb = s_t[:].bitcast(BF16)
+
+        xw = x_sb[:].bitcast(F32)
+        for gp in range(GB // 2):
+            xt = ps_tr.tile([P, 2, 2, P], F32, tag="tr")
+            for a in range(2):
+                g = 2 * gp + a
+                for u in range(2):
+                    nc.tensor.transpose(
+                        out=xt[:, a, u, :], in_=xw[:, 256 * g + u : 256 * (g + 1) : 2], identity=ident_f[:]
+                    )
+            for a in range(2):
+                g = 2 * gp + a
+                nc.vector.tensor_tensor(
+                    out=x_grp[:, g, :, :].rearrange("p r (u e) -> p r u e", e=2),
+                    in0=xt[:, a, :, :].bitcast(BF16).rearrange("p u (r e) -> p r u e", e=2),
+                    in1=s_tb[:, g, :].rearrange("p (u e) -> p u e", e=2).unsqueeze(1).to_broadcast([P, P, 2, 2]),
+                    op=MULT,
+                )
+            nc.vector.quantize_mx(
+                out=x_codes[:, 256 * gp : 256 * (gp + 1)].bitcast(FP8X4),
+                scales=x_pl[:, 256 * gp : 256 * (gp + 1)],
+                in_=x_grp[:, 2 * gp : 2 * gp + 2, :, :].rearrange("p g r t -> p (g r t)"),
+            )
+
+        for i in range(8):
+            bc = ps_tr.tile([P, 1024], BF16, tag="tr")
+            for h in range(2):
+                row = 12 + 2 * i + h
+                nc.tensor.matmul(
+                    out=bc[:, 512 * h : 512 * (h + 1)],
+                    lhsT=ident_b[:, row : row + 1].to_broadcast([P, P]),
+                    rhs=vecs[:],
+                    start=True,
+                    stop=True,
+                )
+            dst = s4_b if i < 4 else bias_b
+            nc.scalar.copy(out=dst[:, 1024 * (i % 4) : 1024 * (i % 4 + 1)], in_=bc[:])
+
+        h1 = []
+        for j in range(GA):
+            h1.append(ps_acc.tile([P, 512], F32, tag="acc", name="h1_%d" % j))
+        for g in range(GB):
+            k = 4 * (g % 4)
+            for j in range(GA):
+                nc.tensor.matmul_mx(
+                    out=h1[j][:],
+                    lhsT=x_codes[:, P * g : P * (g + 1)].bitcast(FP8X4),
+                    lhsT_scale=x_pl[:, P * g : P * (g + 1)],
+                    rhs=b_w[:, g, 512 * j : 512 * (j + 1)].bitcast(FP8X4),
+                    rhs_scale=b_pl[k:P, g // 4, 512 * j : 512 * (j + 1)],
+                    start=(g == 0),
+                    stop=(g == GB - 1),
+                )
+
+        for j in range(GA):
+            nc.scalar.copy(out=h1_sb[:, j, :, :], in_=h1[j][:].rearrange("r (p t) -> r t p", t=4))
+            ht = ps_tr.tile([P, 4, P], F32, tag="tr")
+            for t in range(4):
+                nc.tensor.transpose(out=ht[:, t, :], in_=h1_sb[:, j, t, :], identity=ident_f[:])
+            nc.vector.tensor_tensor(
+                out=h_grp[:, j, :, :],
+                in0=ht[:].rearrange("p t r -> p r t"),
+                in1=s_tb[:, 8 + j, :].unsqueeze(1).to_broadcast([P, P, 4]),
+                op=MULT,
+            )
+            nc.vector.quantize_mx(
+                out=h_codes[:, P * j : P * (j + 1)].bitcast(FP8X4),
+                scales=h_pl[:, P * j : P * (j + 1)],
+                in_=h_grp[:, j, :, :].rearrange("p r t -> p (r t)"),
+            )
+
+        c0 = 0
+        for w in A_CHUNKS:
+            for n0 in range(c0, c0 + w, 512):
+                n = min(512, w)
+                acc = ps_acc.tile([P, n], F32, tag="acc")
+                for g in range(GA):
+                    nc.tensor.matmul_mx(
+                        out=acc[:],
+                        lhsT=h_codes[:, P * g : P * (g + 1)].bitcast(FP8X4),
+                        lhsT_scale=h_pl[:, P * g : P * (g + 1)],
+                        rhs=a_w[:, g, n0 : n0 + n].bitcast(FP8X4),
+                        rhs_scale=a_pl[4 * g : P, n0 : n0 + n],
+                        start=(g == 0),
+                        stop=(g == GA - 1),
+                    )
+                t1 = work.tile([P, n], F32, tag="t1")
+                nc.vector.tensor_tensor(out=t1[:], in0=acc[:], in1=s4_b[:, n0 : n0 + n], op=MULT)
+                nc.gpsimd.tensor_tensor(out=o_sb[:, n0 : n0 + n], in0=t1[:], in1=bias_b[:, n0 : n0 + n], op=ADD)
+                nc.sync.dma_start(out=of[:, n0 : n0 + n], in_=o_sb[:, n0 : n0 + n])
+            c0 += w

@@ -66,14 +66,14 @@ def tile_doublebinarylinear_w_kernel(
         nc.scalar.dma_start(out=vecs[20:28, :], in_=bias.rearrange("(g n) -> g n", n=512))
         for s in range(2):
             for q in (0, 2, 1, 3):
-                nc.sync.dma_start(
-                    out=b_pl[32 * q : 32 * q + 16, s, :].bitcast(I32),
-                    in_=B_scales[4 * s : 4 * s + 4, 4 * q : 4 * q + 4, :].bitcast(I32),
+                nc.gpsimd.dma_start(
+                    out=b_pl[32 * q : 32 * q + 16, s, :].bitcast(F32),
+                    in_=B_scales[4 * s : 4 * s + 4, 4 * q : 4 * q + 4, :].bitcast(F32),
                 )
         for q in (0, 2, 1, 3):
-            nc.sync.dma_start(
-                out=a_pl[32 * q : 32 * q + 16, :].bitcast(I32),
-                in_=A_scales[:, 4 * q : 4 * q + 4, :].bitcast(I32),
+            nc.gpsimd.dma_start(
+                out=a_pl[32 * q : 32 * q + 16, :].bitcast(F32),
+                in_=A_scales[:, 4 * q : 4 * q + 4, :].bitcast(F32),
             )
         for g in range(GB):
             nc.sync.dma_start(out=b_w[:, g, :], in_=B_words[g].rearrange("p n t -> p (n t)").bitcast(I32))

@@ -17,7 +17,12 @@ GB = IN_DIM // 512
 GA = MID_DIM // 512
 FLOPS = 2 * P * IN_DIM * MID_DIM + 2 * P * MID_DIM * OUT_DIM
 
-A_CHUNKS = [1024, 1024, 1024, 512, 256, 256]
+A_PIECES = (
+    [(g, 0, 2048) for g in range(4)]
+    + [(g, 2048, 3072) for g in range(4)]
+    + [(g, 3072, 4096) for g in range(3)]
+    + [(3, 3072, 3584), (3, 3584, 4096)]
+)
 
 
 def tile_doublebinarylinear_w_kernel(
@@ -28,7 +33,7 @@ def tile_doublebinarylinear_w_kernel(
     of = out.flatten_outer_dims()
     with ExitStack() as ctx:
         keep = ctx.enter_context(tc.tile_pool(name="keep", bufs=1))
-        work = ctx.enter_context(tc.tile_pool(name="work", bufs=3))
+        work = ctx.enter_context(tc.tile_pool(name="work", bufs=4))
         ps_acc = ctx.enter_context(tc.psum_pool(name="ps_acc", bufs=4))
         ps_tr = ctx.enter_context(tc.psum_pool(name="ps_tr", bufs=4))
 
@@ -58,32 +63,30 @@ def tile_doublebinarylinear_w_kernel(
         make_identity(nc, ident_f[:])
         make_identity(nc, ident_b[:])
 
-        for h in range(2):
-            nc.sync.dma_start(out=x_sb[:, 2048 * h : 2048 * (h + 1)], in_=xf[:, 2048 * h : 2048 * (h + 1)])
         nc.scalar.dma_start(out=vecs[0:8, :], in_=scaling0.rearrange("(g n) -> g n", n=512))
         nc.scalar.dma_start(out=vecs[8:12, :], in_=scaling2.rearrange("(g n) -> g n", n=512))
         nc.scalar.dma_start(out=vecs[12:20, :], in_=scaling4.rearrange("(g n) -> g n", n=512))
         nc.scalar.dma_start(out=vecs[20:28, :], in_=bias.rearrange("(g n) -> g n", n=512))
+        for h in range(2):
+            nc.sync.dma_start(out=x_sb[:, 2048 * h : 2048 * (h + 1)], in_=xf[:, 2048 * h : 2048 * (h + 1)])
         for s in range(2):
             for q in (0, 2, 1, 3):
-                nc.gpsimd.dma_start(
-                    out=b_pl[32 * q : 32 * q + 16, s, :].bitcast(F32),
-                    in_=B_scales[4 * s : 4 * s + 4, 4 * q : 4 * q + 4, :].bitcast(F32),
+                nc.sync.dma_start(
+                    out=b_pl[32 * q : 32 * q + 16, s, :].bitcast(I32),
+                    in_=B_scales[4 * s : 4 * s + 4, 4 * q : 4 * q + 4, :].bitcast(I32),
                 )
         for q in (0, 2, 1, 3):
-            nc.gpsimd.dma_start(
-                out=a_pl[32 * q : 32 * q + 16, :].bitcast(F32),
-                in_=A_scales[:, 4 * q : 4 * q + 4, :].bitcast(F32),
+            nc.sync.dma_start(
+                out=a_pl[32 * q : 32 * q + 16, :].bitcast(I32),
+                in_=A_scales[:, 4 * q : 4 * q + 4, :].bitcast(I32),
             )
         for g in range(GB):
             nc.sync.dma_start(out=b_w[:, g, :], in_=B_words[g].rearrange("p n t -> p (n t)").bitcast(I32))
-        c0 = 0
-        for w in A_CHUNKS:
+        for g, lo, hi in A_PIECES:
             nc.sync.dma_start(
-                out=a_w[:, :, c0 : c0 + w],
-                in_=A_words[:, :, c0 : c0 + w, :].rearrange("g p n t -> p g (n t)").bitcast(I32),
+                out=a_w[:, g, lo:hi],
+                in_=A_words[g, :, lo:hi, :].rearrange("p n t -> p (n t)").bitcast(I32),
             )
-            c0 += w
 
         vw = vecs[:].bitcast(F32)
         vt = ps_tr.tile([P, 2, P], F32, tag="tr")
@@ -162,23 +165,46 @@ def tile_doublebinarylinear_w_kernel(
                 in_=h_grp[:, j, :, :].rearrange("p r t -> p (r t)"),
             )
 
-        c0 = 0
-        for w in A_CHUNKS:
-            for n0 in range(c0, c0 + w, 512):
-                n = min(512, w)
-                acc = ps_acc.tile([P, n], F32, tag="acc")
-                for g in range(GA):
+        def passes(accs, cs, gs):
+            for g in gs:
+                for c in cs:
                     nc.tensor.matmul_mx(
-                        out=acc[:],
+                        out=accs[c][:],
                         lhsT=h_codes[:, P * g : P * (g + 1)].bitcast(FP8X4),
                         lhsT_scale=h_pl[:, P * g : P * (g + 1)],
-                        rhs=a_w[:, g, n0 : n0 + n].bitcast(FP8X4),
-                        rhs_scale=a_pl[4 * g : P, n0 : n0 + n],
+                        rhs=a_w[:, g, 512 * c : 512 * (c + 1)].bitcast(FP8X4),
+                        rhs_scale=a_pl[4 * g : P, 512 * c : 512 * (c + 1)],
                         start=(g == 0),
                         stop=(g == GA - 1),
                     )
-                t1 = work.tile([P, n], F32, tag="t1")
-                nc.vector.tensor_tensor(out=t1[:], in0=acc[:], in1=s4_b[:, n0 : n0 + n], op=MULT)
-                nc.gpsimd.tensor_tensor(out=o_sb[:, n0 : n0 + n], in0=t1[:], in1=bias_b[:, n0 : n0 + n], op=ADD)
-                nc.sync.dma_start(out=of[:, n0 : n0 + n], in_=o_sb[:, n0 : n0 + n])
-            c0 += w
+
+        def epilogue(accs, c, cut):
+            n0 = 512 * c
+            t1 = work.tile([P, 512], F32, tag="t1")
+            nc.vector.tensor_tensor(out=t1[:], in0=accs[c][:], in1=s4_b[:, n0 : n0 + 512], op=MULT)
+            nc.gpsimd.tensor_tensor(
+                out=o_sb[:, n0 : n0 + cut], in0=t1[:, 0:cut], in1=bias_b[:, n0 : n0 + cut], op=ADD
+            )
+            if cut < 512:
+                nc.vector.tensor_tensor(
+                    out=o_sb[:, n0 + cut : n0 + 512], in0=t1[:, cut:512], in1=bias_b[:, n0 + cut : n0 + 512], op=ADD
+                )
+
+        accs = {}
+        for c in range(4):
+            accs[c] = ps_acc.tile([P, 512], F32, tag="acc", name="acc_%d" % c)
+        passes(accs, range(4), range(4))
+        for c in range(4):
+            epilogue(accs, c, 512)
+        nc.sync.dma_start(out=of[:, 0:2048], in_=o_sb[:, 0:2048])
+        for c in range(4, 8):
+            accs[c] = ps_tr.tile([P, 512], F32, tag="tr", name="acc_%d" % c)
+        passes(accs, (4, 5), range(4))
+        for c in (4, 5):
+            epilogue(accs, c, 512)
+        nc.sync.dma_start(out=of[:, 2048:3072], in_=o_sb[:, 2048:3072])
+        passes(accs, (6, 7), range(3))
+        for c in (6, 7):
+            passes(accs, (c,), (3,))
+            epilogue(accs, c, 192)
+            nc.sync.dma_start(out=of[:, 512 * c : 512 * (c + 1)], in_=o_sb[:, 512 * c : 512 * (c + 1)])

@@ -20,8 +20,8 @@ FLOPS = 2 * P * IN_DIM * MID_DIM + 2 * P * MID_DIM * OUT_DIM
 A_PIECES = (
     [(g, 0, 2048) for g in range(4)]
     + [(g, 2048, 3072) for g in range(4)]
-    + [(g, 3072, 4096) for g in range(3)]
-    + [(3, 3072, 3584), (3, 3584, 4096)]
+    + [(g, 3072, 4096) for g in range(2)]
+    + [(2, 3072, 3584), (3, 3072, 3584), (2, 3584, 4096), (3, 3584, 4096)]
 )
 
 
@@ -178,33 +178,27 @@ def tile_doublebinarylinear_w_kernel(
                         stop=(g == GA - 1),
                     )
 
-        def epilogue(accs, c, cut):
+        def epilogue(accs, c, adder):
             n0 = 512 * c
             t1 = work.tile([P, 512], F32, tag="t1")
             nc.vector.tensor_tensor(out=t1[:], in0=accs[c][:], in1=s4_b[:, n0 : n0 + 512], op=MULT)
-            nc.gpsimd.tensor_tensor(
-                out=o_sb[:, n0 : n0 + cut], in0=t1[:, 0:cut], in1=bias_b[:, n0 : n0 + cut], op=ADD
-            )
-            if cut < 512:
-                nc.vector.tensor_tensor(
-                    out=o_sb[:, n0 + cut : n0 + 512], in0=t1[:, cut:512], in1=bias_b[:, n0 + cut : n0 + 512], op=ADD
-                )
+            adder.tensor_tensor(out=o_sb[:, n0 : n0 + 512], in0=t1[:], in1=bias_b[:, n0 : n0 + 512], op=ADD)
 
         accs = {}
         for c in range(4):
             accs[c] = ps_acc.tile([P, 512], F32, tag="acc", name="acc_%d" % c)
         passes(accs, range(4), range(4))
         for c in range(4):
-            epilogue(accs, c, 512)
+            epilogue(accs, c, nc.gpsimd if c % 2 == 0 else nc.vector)
         nc.sync.dma_start(out=of[:, 0:2048], in_=o_sb[:, 0:2048])
         for c in range(4, 8):
             accs[c] = ps_tr.tile([P, 512], F32, tag="tr", name="acc_%d" % c)
         passes(accs, (4, 5), range(4))
         for c in (4, 5):
-            epilogue(accs, c, 512)
+            epilogue(accs, c, nc.gpsimd if c % 2 == 0 else nc.vector)
         nc.sync.dma_start(out=of[:, 2048:3072], in_=o_sb[:, 2048:3072])
-        passes(accs, (6, 7), range(3))
+        passes(accs, (6, 7), range(2))
         for c in (6, 7):
-            passes(accs, (c,), (3,))
-            epilogue(accs, c, 192)
+            passes(accs, (c,), (2, 3))
+            epilogue(accs, c, nc.vector)
             nc.sync.dma_start(out=of[:, 512 * c : 512 * (c + 1)], in_=o_sb[:, 512 * c : 512 * (c + 1)])

@@ -178,27 +178,39 @@ def tile_doublebinarylinear_w_kernel(
                         stop=(g == GA - 1),
                     )
 
-        def epilogue(accs, c, adder):
+        def scale(accs, c):
+            t1 = work.tile([P, 512], F32, tag="t1", name="t1_%d" % c)
             n0 = 512 * c
-            t1 = work.tile([P, 512], F32, tag="t1")
             nc.vector.tensor_tensor(out=t1[:], in0=accs[c][:], in1=s4_b[:, n0 : n0 + 512], op=MULT)
-            adder.tensor_tensor(out=o_sb[:, n0 : n0 + 512], in0=t1[:], in1=bias_b[:, n0 : n0 + 512], op=ADD)
+            return t1
 
+        def add_bias(t1, c):
+            n0 = 512 * c
+            nc.vector.tensor_tensor(out=o_sb[:, n0 : n0 + 512], in0=t1[:], in1=bias_b[:, n0 : n0 + 512], op=ADD)
+
+        def epilogue(accs, cs):
+            prev = None
+            for c in cs:
+                t1 = scale(accs, c)
+                if prev is not None:
+                    add_bias(*prev)
+                prev = (t1, c)
+            add_bias(*prev)
+
+        ctx.enter_context(tc.manual_schedule(engines={mybir.EngineType.DVE}))
         accs = {}
         for c in range(4):
             accs[c] = ps_acc.tile([P, 512], F32, tag="acc", name="acc_%d" % c)
         passes(accs, range(4), range(4))
-        for c in range(4):
-            epilogue(accs, c, nc.gpsimd if c % 2 == 0 else nc.vector)
+        epilogue(accs, range(4))
         nc.sync.dma_start(out=of[:, 0:2048], in_=o_sb[:, 0:2048])
         for c in range(4, 8):
             accs[c] = ps_tr.tile([P, 512], F32, tag="tr", name="acc_%d" % c)
         passes(accs, (4, 5), range(4))
-        for c in (4, 5):
-            epilogue(accs, c, nc.gpsimd if c % 2 == 0 else nc.vector)
+        epilogue(accs, (4, 5))
         nc.sync.dma_start(out=of[:, 2048:3072], in_=o_sb[:, 2048:3072])
         passes(accs, (6, 7), range(2))
         for c in (6, 7):
             passes(accs, (c,), (2, 3))
-            epilogue(accs, c, nc.vector)
+            epilogue(accs, (c,))
             nc.sync.dma_start(out=of[:, 512 * c : 512 * (c + 1)], in_=o_sb[:, 512 * c : 512 * (c + 1)])

@@ -17,11 +17,11 @@ GB = IN_DIM // 512
 GA = MID_DIM // 512
 FLOPS = 2 * P * IN_DIM * MID_DIM + 2 * P * MID_DIM * OUT_DIM
 
+B_PIECES = [(0, 2), (2, 4), (4, 6), (6, 7), (7, 8)]
 A_PIECES = (
-    [(g, 0, 2048) for g in range(4)]
-    + [(g, 2048, 3072) for g in range(4)]
-    + [(g, 3072, 4096) for g in range(2)]
-    + [(2, 3072, 3584), (3, 3072, 3584), (2, 3584, 4096), (3, 3584, 4096)]
+    [(g0, g1, lo, lo + w) for lo, w in ((0, 2048), (2048, 1024)) for g0, g1 in ((0, 2), (2, 3), (3, 4))]
+    + [(0, 2, 3072, 4096)]
+    + [(g, g + 1, lo, lo + 512) for lo in (3072, 3584) for g in (2, 3)]
 )
 
 
@@ -57,6 +57,7 @@ def tile_doublebinarylinear_w_kernel(
         h_pl = keep.tile([P, GA * P], U8, align_bytes=64)
         o_sb = keep.tile([P, OUT_DIM], F32)
 
+        ctx.enter_context(tc.manual_schedule(engines={mybir.EngineType.DVE, mybir.EngineType.SP}))
         nc.vector.memset(vecs[:], 0.0)
         nc.vector.memset(b_pl[:].bitcast(I32), 0)
         nc.vector.memset(a_pl[:].bitcast(I32), 0)
@@ -67,25 +68,27 @@ def tile_doublebinarylinear_w_kernel(
         nc.scalar.dma_start(out=vecs[8:12, :], in_=scaling2.rearrange("(g n) -> g n", n=512))
         nc.scalar.dma_start(out=vecs[12:20, :], in_=scaling4.rearrange("(g n) -> g n", n=512))
         nc.scalar.dma_start(out=vecs[20:28, :], in_=bias.rearrange("(g n) -> g n", n=512))
-        for h in range(2):
-            nc.sync.dma_start(out=x_sb[:, 2048 * h : 2048 * (h + 1)], in_=xf[:, 2048 * h : 2048 * (h + 1)])
-        for s in range(2):
-            for q in (0, 2, 1, 3):
+        nc.sync.dma_start(out=x_sb[:], in_=xf)
+        for half in ((2, 3), (0, 1)):
+            for s in range(2):
+                for q in half:
+                    nc.sync.dma_start(
+                        out=b_pl[32 * q : 32 * q + 16, s, :].bitcast(I32),
+                        in_=B_scales[4 * s : 4 * s + 4, 4 * q : 4 * q + 4, :].bitcast(I32),
+                    )
+            for q in half:
                 nc.sync.dma_start(
-                    out=b_pl[32 * q : 32 * q + 16, s, :].bitcast(I32),
-                    in_=B_scales[4 * s : 4 * s + 4, 4 * q : 4 * q + 4, :].bitcast(I32),
+                    out=a_pl[32 * q : 32 * q + 16, :].bitcast(I32),
+                    in_=A_scales[:, 4 * q : 4 * q + 4, :].bitcast(I32),
                 )
-        for q in (0, 2, 1, 3):
+        for g0, g1 in B_PIECES:
             nc.sync.dma_start(
-                out=a_pl[32 * q : 32 * q + 16, :].bitcast(I32),
-                in_=A_scales[:, 4 * q : 4 * q + 4, :].bitcast(I32),
+                out=b_w[:, g0:g1, :], in_=B_words[g0:g1].rearrange("g p n t -> p g (n t)").bitcast(I32)
             )
-        for g in range(GB):
-            nc.sync.dma_start(out=b_w[:, g, :], in_=B_words[g].rearrange("p n t -> p (n t)").bitcast(I32))
-        for g, lo, hi in A_PIECES:
+        for g0, g1, lo, hi in A_PIECES:
             nc.sync.dma_start(
-                out=a_w[:, g, lo:hi],
-                in_=A_words[g, :, lo:hi, :].rearrange("p n t -> p (n t)").bitcast(I32),
+                out=a_w[:, g0:g1, lo:hi],
+                in_=A_words[g0:g1, :, lo:hi, :].rearrange("g p n t -> p g (n t)").bitcast(I32),
             )
 
         vw = vecs[:].bitcast(F32)
@@ -197,7 +200,6 @@ def tile_doublebinarylinear_w_kernel(
                 prev = (t1, c)
             add_bias(*prev)
 
-        ctx.enter_context(tc.manual_schedule(engines={mybir.EngineType.DVE}))
         accs = {}
         for c in range(4):
             accs[c] = ps_acc.tile([P, 512], F32, tag="acc", name="acc_%d" % c)

@@ -20,8 +20,7 @@ FLOPS = 2 * P * IN_DIM * MID_DIM + 2 * P * MID_DIM * OUT_DIM
 B_PIECES = [(0, 2), (2, 4), (4, 6), (6, 7), (7, 8)]
 A_PIECES = (
     [(g0, g1, lo, lo + w) for lo, w in ((0, 2048), (2048, 1024)) for g0, g1 in ((0, 2), (2, 3), (3, 4))]
-    + [(0, 2, 3072, 4096)]
-    + [(g, g + 1, lo, lo + 512) for lo in (3072, 3584) for g in (2, 3)]
+    + [(0, 2, 3072, 3584), (2, 4, 3072, 3584), (0, 3, 3584, 4096), (3, 4, 3584, 4096)]
 )
 
 
@@ -168,51 +167,56 @@ def tile_doublebinarylinear_w_kernel(
                 in_=h_grp[:, j, :, :].rearrange("p r t -> p (r t)"),
             )
 
-        def passes(accs, cs, gs):
+        def passes(accs, spans, gs):
             for g in gs:
-                for c in cs:
+                for lo, hi in spans:
                     nc.tensor.matmul_mx(
-                        out=accs[c][:],
+                        out=accs[lo][:],
                         lhsT=h_codes[:, P * g : P * (g + 1)].bitcast(FP8X4),
                         lhsT_scale=h_pl[:, P * g : P * (g + 1)],
-                        rhs=a_w[:, g, 512 * c : 512 * (c + 1)].bitcast(FP8X4),
-                        rhs_scale=a_pl[4 * g : P, 512 * c : 512 * (c + 1)],
+                        rhs=a_w[:, g, lo:hi].bitcast(FP8X4),
+                        rhs_scale=a_pl[4 * g : P, lo:hi],
                         start=(g == 0),
                         stop=(g == GA - 1),
                     )
 
-        def scale(accs, c):
-            t1 = work.tile([P, 512], F32, tag="t1", name="t1_%d" % c)
-            n0 = 512 * c
-            nc.vector.tensor_tensor(out=t1[:], in0=accs[c][:], in1=s4_b[:, n0 : n0 + 512], op=MULT)
+        def scale(accs, span):
+            lo, hi = span
+            t1 = work.tile([P, hi - lo], F32, tag="t1", name="t1_%d" % lo)
+            nc.vector.tensor_tensor(out=t1[:], in0=accs[lo][:], in1=s4_b[:, lo:hi], op=MULT)
             return t1
 
-        def add_bias(t1, c):
-            n0 = 512 * c
-            nc.vector.tensor_tensor(out=o_sb[:, n0 : n0 + 512], in0=t1[:], in1=bias_b[:, n0 : n0 + 512], op=ADD)
+        def add_bias(t1, span):
+            lo, hi = span
+            nc.vector.tensor_tensor(out=o_sb[:, lo:hi], in0=t1[:], in1=bias_b[:, lo:hi], op=ADD)
 
-        def epilogue(accs, cs):
+        def epilogue(accs, spans):
             prev = None
-            for c in cs:
-                t1 = scale(accs, c)
+            for span in spans:
+                t1 = scale(accs, span)
                 if prev is not None:
                     add_bias(*prev)
-                prev = (t1, c)
+                prev = (t1, span)
             add_bias(*prev)
 
+        def store(lo, hi):
+            nc.sync.dma_start(out=of[:, lo:hi], in_=o_sb[:, lo:hi])
+
         accs = {}
-        for c in range(4):
-            accs[c] = ps_acc.tile([P, 512], F32, tag="acc", name="acc_%d" % c)
-        passes(accs, range(4), range(4))
-        epilogue(accs, range(4))
-        nc.sync.dma_start(out=of[:, 0:2048], in_=o_sb[:, 0:2048])
-        for c in range(4, 8):
-            accs[c] = ps_tr.tile([P, 512], F32, tag="tr", name="acc_%d" % c)
-        passes(accs, (4, 5), range(4))
-        epilogue(accs, (4, 5))
-        nc.sync.dma_start(out=of[:, 2048:3072], in_=o_sb[:, 2048:3072])
-        passes(accs, (6, 7), range(2))
-        for c in (6, 7):
-            passes(accs, (c,), (2, 3))
-            epilogue(accs, (c,))
-            nc.sync.dma_start(out=of[:, 512 * c : 512 * (c + 1)], in_=o_sb[:, 512 * c : 512 * (c + 1)])
+        spans = [(lo, lo + 512) for lo in range(0, 3584, 512)] + [(3584, 3840), (3840, 4096)]
+        for i, (lo, hi) in enumerate(spans):
+            pool, tag = (ps_tr, "tr") if 4 <= i < 8 else (ps_acc, "acc")
+            accs[lo] = pool.tile([P, hi - lo], F32, tag=tag, name="acc_%d" % lo)
+        passes(accs, spans[0:4], range(4))
+        epilogue(accs, spans[0:4])
+        store(0, 2048)
+        passes(accs, spans[4:6], range(4))
+        epilogue(accs, spans[4:6])
+        store(2048, 3072)
+        passes(accs, spans[6:7], range(4))
+        epilogue(accs, spans[6:7])
+        store(3072, 3584)
+        passes(accs, spans[7:9], range(4))
+        epilogue(accs, spans[7:9])
+        store(3584, 3840)
+        store(3840, 4096)

@@ -17,7 +17,6 @@ GB = IN_DIM // 512
 GA = MID_DIM // 512
 FLOPS = 2 * P * IN_DIM * MID_DIM + 2 * P * MID_DIM * OUT_DIM
 
-B_PIECES = [(0, 2), (2, 4), (4, 6), (6, 7), (7, 8)]
 A_PIECES = (
     [(g0, g1, lo, lo + w) for lo, w in ((0, 2048), (2048, 1024)) for g0, g1 in ((0, 2), (2, 3), (3, 4))]
     + [(0, 2, 3072, 3584), (2, 4, 3072, 3584), (0, 3, 3584, 4096), (3, 4, 3584, 4096)]
@@ -38,6 +37,7 @@ def tile_doublebinarylinear_w_kernel(
 
         x_sb = keep.tile([P, IN_DIM], BF16, align_bytes=64)
         vecs = keep.tile([P, 512], BF16, align_bytes=64)
+        rows = keep.tile([P, 512], BF16, align_bytes=64)
         b_pl = keep.tile([P, 2, MID_DIM], U8, align_bytes=64)
         a_pl = keep.tile([P, OUT_DIM], U8, align_bytes=64)
         b_w = keep.tile([P, GB, MID_DIM], I32, align_bytes=64)
@@ -60,30 +60,45 @@ def tile_doublebinarylinear_w_kernel(
         nc.vector.memset(vecs[:], 0.0)
         nc.vector.memset(b_pl[:].bitcast(I32), 0)
         nc.vector.memset(a_pl[:].bitcast(I32), 0)
+        nc.vector.memset(rows[:], 0.0)
         make_identity(nc, ident_f[:])
         make_identity(nc, ident_b[:])
 
-        nc.scalar.dma_start(out=vecs[0:8, :], in_=scaling0.rearrange("(g n) -> g n", n=512))
-        nc.scalar.dma_start(out=vecs[8:12, :], in_=scaling2.rearrange("(g n) -> g n", n=512))
-        nc.scalar.dma_start(out=vecs[12:20, :], in_=scaling4.rearrange("(g n) -> g n", n=512))
-        nc.scalar.dma_start(out=vecs[20:28, :], in_=bias.rearrange("(g n) -> g n", n=512))
-        nc.sync.dma_start(out=x_sb[:], in_=xf)
-        for half in ((2, 3), (0, 1)):
-            for s in range(2):
-                for q in half:
-                    nc.sync.dma_start(
-                        out=b_pl[32 * q : 32 * q + 16, s, :].bitcast(I32),
-                        in_=B_scales[4 * s : 4 * s + 4, 4 * q : 4 * q + 4, :].bitcast(I32),
-                    )
-            for q in half:
+        def load_b_words(g0, g1):
+            nc.sync.dma_start(
+                out=b_w[:, g0:g1, :], in_=B_words[g0:g1].rearrange("g p n t -> p g (n t)").bitcast(I32)
+            )
+
+        def load_b_scales(s, quadrants):
+            for q in quadrants:
+                nc.sync.dma_start(
+                    out=b_pl[32 * q : 32 * q + 16, s, :].bitcast(I32),
+                    in_=B_scales[4 * s : 4 * s + 4, 4 * q : 4 * q + 4, :].bitcast(I32),
+                )
+
+        def load_a_scales(quadrants):
+            for q in quadrants:
                 nc.sync.dma_start(
                     out=a_pl[32 * q : 32 * q + 16, :].bitcast(I32),
                     in_=A_scales[:, 4 * q : 4 * q + 4, :].bitcast(I32),
                 )
-        for g0, g1 in B_PIECES:
-            nc.sync.dma_start(
-                out=b_w[:, g0:g1, :], in_=B_words[g0:g1].rearrange("g p n t -> p g (n t)").bitcast(I32)
-            )
+
+        nc.sync.dma_start(out=x_sb[:], in_=xf)
+        nc.sync.dma_start(out=vecs[0:8, :], in_=scaling0.rearrange("(g n) -> g n", n=512))
+        nc.sync.dma_start(out=vecs[8:12, :], in_=scaling2.rearrange("(g n) -> g n", n=512))
+        for s in range(2):
+            load_b_scales(s, (2, 3))
+        load_a_scales((2, 3))
+        load_b_scales(0, (0, 1))
+        load_b_words(0, 2)
+        load_b_scales(1, (0, 1))
+        load_a_scales((0, 1))
+        load_b_words(2, 4)
+        nc.sync.dma_start(out=rows[0:8, :], in_=scaling4.rearrange("(g n) -> g n", n=512))
+        nc.sync.dma_start(out=rows[8:16, :], in_=bias.rearrange("(g n) -> g n", n=512))
+        load_b_words(4, 6)
+        load_b_words(6, 7)
+        load_b_words(7, 8)
         for g0, g1, lo, hi in A_PIECES:
             nc.sync.dma_start(
                 out=a_w[:, g0:g1, lo:hi],
@@ -120,24 +135,28 @@ def tile_doublebinarylinear_w_kernel(
                 in_=x_grp[:, 2 * gp : 2 * gp + 2, :, :].rearrange("p g r t -> p (g r t)"),
             )
 
-        for i in range(8):
-            bc = ps_tr.tile([P, 1024], BF16, tag="tr")
-            for h in range(2):
-                row = 12 + 2 * i + h
-                nc.tensor.matmul(
-                    out=bc[:, 512 * h : 512 * (h + 1)],
-                    lhsT=ident_b[:, row : row + 1].to_broadcast([P, P]),
-                    rhs=vecs[:],
-                    start=True,
-                    stop=True,
-                )
-            dst = s4_b if i < 4 else bias_b
-            nc.scalar.copy(out=dst[:, 1024 * (i % 4) : 1024 * (i % 4 + 1)], in_=bc[:])
+        def spread_rows():
+            for i in range(8):
+                bc = ps_tr.tile([P, 1024], BF16, tag="tr")
+                for h in range(2):
+                    row = 2 * i + h
+                    nc.tensor.matmul(
+                        out=bc[:, 512 * h : 512 * (h + 1)],
+                        lhsT=ident_b[:, row : row + 1].to_broadcast([P, P]),
+                        rhs=rows[:],
+                        start=True,
+                        stop=True,
+                    )
+                dst = s4_b if i < 4 else bias_b
+                copy = nc.scalar.copy if i % 2 == 0 else nc.vector.tensor_copy
+                copy(out=dst[:, 1024 * (i % 4) : 1024 * (i % 4 + 1)], in_=bc[:])
 
         h1 = []
         for j in range(GA):
             h1.append(ps_acc.tile([P, 512], F32, tag="acc", name="h1_%d" % j))
         for g in range(GB):
+            if g == 4:
+                spread_rows()
             k = 4 * (g % 4)
             for j in range(GA):
                 nc.tensor.matmul_mx(

from contextlib import ExitStack

import concourse.mybir as mybir
from concourse.masks import make_identity

F32 = mybir.dt.float32
BF16 = mybir.dt.bfloat16
I32 = mybir.dt.int32
U8 = mybir.dt.uint8
FP8X4 = mybir.dt.float8_e4m3fn_x4
MULT = mybir.AluOpType.mult
ADD = mybir.AluOpType.add

P = 128
IN_DIM, MID_DIM, OUT_DIM = 4096, 2048, 4096
GB = IN_DIM // 512
GA = MID_DIM // 512
FLOPS = 2 * P * IN_DIM * MID_DIM + 2 * P * MID_DIM * OUT_DIM

A_PIECES = (
    [(g0, g1, lo, lo + w) for lo, w in ((0, 2048), (2048, 1024)) for g0, g1 in ((0, 2), (2, 3), (3, 4))]
    + [(0, 2, 3072, 3584), (2, 4, 3072, 3584), (0, 3, 3584, 4096), (3, 4, 3584, 4096)]
)


def tile_doublebinarylinear_w_kernel(
    tc, x, scaling0, B_words, B_scales, scaling2, A_words, A_scales, scaling4, bias, out
):
    nc = tc.nc
    xf = x.flatten_outer_dims()
    of = out.flatten_outer_dims()
    with ExitStack() as ctx:
        keep = ctx.enter_context(tc.tile_pool(name="keep", bufs=1))
        work = ctx.enter_context(tc.tile_pool(name="work", bufs=4))
        ps_acc = ctx.enter_context(tc.psum_pool(name="ps_acc", bufs=4))
        ps_tr = ctx.enter_context(tc.psum_pool(name="ps_tr", bufs=4))

        x_sb = keep.tile([P, IN_DIM], BF16, align_bytes=64)
        vecs = keep.tile([P, 512], BF16, align_bytes=64)
        rows = keep.tile([P, 512], BF16, align_bytes=64)
        b_pl = keep.tile([P, 2, MID_DIM], U8, align_bytes=64)
        a_pl = keep.tile([P, OUT_DIM], U8, align_bytes=64)
        b_w = keep.tile([P, GB, MID_DIM], I32, align_bytes=64)
        a_w = keep.tile([P, GA, OUT_DIM], I32, align_bytes=64)
        ident_f = keep.tile([P, P], F32)
        ident_b = keep.tile([P, P], BF16)
        s_t = keep.tile([P, 12, 2], F32)
        x_grp = keep.tile([P, GB, P, 4], BF16, align_bytes=64)
        x_codes = keep.tile([P, GB * P], I32, align_bytes=64)
        x_pl = keep.tile([P, GB * P], U8, align_bytes=64)
        s4_b = keep.tile([P, OUT_DIM], BF16)
        bias_b = keep.tile([P, OUT_DIM], BF16)
        h1_sb = keep.tile([P, GA, 4, P], F32)
        h_grp = keep.tile([P, GA, P, 4], BF16, align_bytes=64)
        h_codes = keep.tile([P, GA * P], I32, align_bytes=64)
        h_pl = keep.tile([P, GA * P], U8, align_bytes=64)
        o_sb = keep.tile([P, OUT_DIM], F32)

        ctx.enter_context(tc.manual_schedule(engines={mybir.EngineType.DVE, mybir.EngineType.SP}))
        nc.vector.memset(vecs[:], 0.0)
        nc.vector.memset(b_pl[:].bitcast(I32), 0)
        nc.vector.memset(a_pl[:].bitcast(I32), 0)
        nc.vector.memset(rows[:], 0.0)
        make_identity(nc, ident_f[:])
        make_identity(nc, ident_b[:])

        def load_b_words(g0, g1):
            nc.sync.dma_start(
                out=b_w[:, g0:g1, :], in_=B_words[g0:g1].rearrange("g p n t -> p g (n t)").bitcast(I32)
            )

        def load_b_scales(s, quadrants):
            for q in quadrants:
                nc.sync.dma_start(
                    out=b_pl[32 * q : 32 * q + 16, s, :].bitcast(I32),
                    in_=B_scales[4 * s : 4 * s + 4, 4 * q : 4 * q + 4, :].bitcast(I32),
                )

        def load_a_scales(quadrants):
            for q in quadrants:
                nc.sync.dma_start(
                    out=a_pl[32 * q : 32 * q + 16, :].bitcast(I32),
                    in_=A_scales[:, 4 * q : 4 * q + 4, :].bitcast(I32),
                )

        nc.sync.dma_start(out=x_sb[:], in_=xf)
        nc.sync.dma_start(out=vecs[0:8, :], in_=scaling0.rearrange("(g n) -> g n", n=512))
        nc.sync.dma_start(out=vecs[8:12, :], in_=scaling2.rearrange("(g n) -> g n", n=512))
        for s in range(2):
            load_b_scales(s, (2, 3))
        load_a_scales((2, 3))
        load_b_scales(0, (0, 1))
        load_b_words(0, 2)
        load_b_scales(1, (0, 1))
        load_a_scales((0, 1))
        load_b_words(2, 4)
        nc.sync.dma_start(out=rows[0:8, :], in_=scaling4.rearrange("(g n) -> g n", n=512))
        nc.sync.dma_start(out=rows[8:16, :], in_=bias.rearrange("(g n) -> g n", n=512))
        load_b_words(4, 6)
        load_b_words(6, 7)
        load_b_words(7, 8)
        for g0, g1, lo, hi in A_PIECES:
            nc.sync.dma_start(
                out=a_w[:, g0:g1, lo:hi],
                in_=A_words[g0:g1, :, lo:hi, :].rearrange("g p n t -> p g (n t)").bitcast(I32),
            )

        vw = vecs[:].bitcast(F32)
        vt = ps_tr.tile([P, 2, P], F32, tag="tr")
        for u in range(2):
            nc.tensor.transpose(out=vt[:, u, :], in_=vw[:, u:256:2], identity=ident_f[:])
        nc.vector.tensor_copy(out=s_t[:], in_=vt[:, :, 0:12].rearrange("p u w -> p w u"))
        s_tb = s_t[:].bitcast(BF16)

        xw = x_sb[:].bitcast(F32)
        for gp in range(GB // 2):
            xt = ps_tr.tile([P, 2, 2, P], F32, tag="tr")
            for a in range(2):
                g = 2 * gp + a
                for u in range(2):
                    nc.tensor.transpose(
                        out=xt[:, a, u, :], in_=xw[:, 256 * g + u : 256 * (g + 1) : 2], identity=ident_f[:]
                    )
            for a in range(2):
                g = 2 * gp + a
                nc.vector.tensor_tensor(
                    out=x_grp[:, g, :, :].rearrange("p r (u e) -> p r u e", e=2),
                    in0=xt[:, a, :, :].bitcast(BF16).rearrange("p u (r e) -> p r u e", e=2),
                    in1=s_tb[:, g, :].rearrange("p (u e) -> p u e", e=2).unsqueeze(1).to_broadcast([P, P, 2, 2]),
                    op=MULT,
                )
            nc.vector.quantize_mx(
                out=x_codes[:, 256 * gp : 256 * (gp + 1)].bitcast(FP8X4),
                scales=x_pl[:, 256 * gp : 256 * (gp + 1)],
                in_=x_grp[:, 2 * gp : 2 * gp + 2, :, :].rearrange("p g r t -> p (g r t)"),
            )

        def spread_rows():
            for i in range(8):
                bc = ps_tr.tile([P, 1024], BF16, tag="tr")
                for h in range(2):
                    row = 2 * i + h
                    nc.tensor.matmul(
                        out=bc[:, 512 * h : 512 * (h + 1)],
                        lhsT=ident_b[:, row : row + 1].to_broadcast([P, P]),
                        rhs=rows[:],
                        start=True,
                        stop=True,
                    )
                dst = s4_b if i < 4 else bias_b
                copy = nc.scalar.copy if i % 2 == 0 else nc.vector.tensor_copy
                copy(out=dst[:, 1024 * (i % 4) : 1024 * (i % 4 + 1)], in_=bc[:])

        h1 = []
        for j in range(GA):
            h1.append(ps_acc.tile([P, 512], F32, tag="acc", name="h1_%d" % j))
        for g in range(GB):
            if g == 4:
                spread_rows()
            k = 4 * (g % 4)
            for j in range(GA):
                nc.tensor.matmul_mx(
                    out=h1[j][:],
                    lhsT=x_codes[:, P * g : P * (g + 1)].bitcast(FP8X4),
                    lhsT_scale=x_pl[:, P * g : P * (g + 1)],
                    rhs=b_w[:, g, 512 * j : 512 * (j + 1)].bitcast(FP8X4),
                    rhs_scale=b_pl[k:P, g // 4, 512 * j : 512 * (j + 1)],
                    start=(g == 0),
                    stop=(g == GB - 1),
                )

        for j in range(GA):
            nc.scalar.copy(out=h1_sb[:, j, :, :], in_=h1[j][:].rearrange("r (p t) -> r t p", t=4))
            ht = ps_tr.tile([P, 4, P], F32, tag="tr")
            for t in range(4):
                nc.tensor.transpose(out=ht[:, t, :], in_=h1_sb[:, j, t, :], identity=ident_f[:])
            nc.vector.tensor_tensor(
                out=h_grp[:, j, :, :],
                in0=ht[:].rearrange("p t r -> p r t"),
                in1=s_tb[:, 8 + j, :].unsqueeze(1).to_broadcast([P, P, 4]),
                op=MULT,
            )
            nc.vector.quantize_mx(
                out=h_codes[:, P * j : P * (j + 1)].bitcast(FP8X4),
                scales=h_pl[:, P * j : P * (j + 1)],
                in_=h_grp[:, j, :, :].rearrange("p r t -> p (r t)"),
            )

        def passes(accs, spans, gs):
            for g in gs:
                for lo, hi in spans:
                    nc.tensor.matmul_mx(
                        out=accs[lo][:],
                        lhsT=h_codes[:, P * g : P * (g + 1)].bitcast(FP8X4),
                        lhsT_scale=h_pl[:, P * g : P * (g + 1)],
                        rhs=a_w[:, g, lo:hi].bitcast(FP8X4),
                        rhs_scale=a_pl[4 * g : P, lo:hi],
                        start=(g == 0),
                        stop=(g == GA - 1),
                    )

        def scale(accs, span):
            lo, hi = span
            t1 = work.tile([P, hi - lo], F32, tag="t1", name="t1_%d" % lo)
            nc.vector.tensor_tensor(out=t1[:], in0=accs[lo][:], in1=s4_b[:, lo:hi], op=MULT)
            return t1

        def add_bias(t1, span):
            lo, hi = span
            nc.vector.tensor_tensor(out=o_sb[:, lo:hi], in0=t1[:], in1=bias_b[:, lo:hi], op=ADD)

        def epilogue(accs, spans):
            prev = None
            for span in spans:
                t1 = scale(accs, span)
                if prev is not None:
                    add_bias(*prev)
                prev = (t1, span)
            add_bias(*prev)

        def store(lo, hi):
            nc.sync.dma_start(out=of[:, lo:hi], in_=o_sb[:, lo:hi])

        accs = {}
        spans = [(lo, lo + 512) for lo in range(0, 3584, 512)] + [(3584, 3840), (3840, 4096)]
        for i, (lo, hi) in enumerate(spans):
            pool, tag = (ps_tr, "tr") if 4 <= i < 8 else (ps_acc, "acc")
            accs[lo] = pool.tile([P, hi - lo], F32, tag=tag, name="acc_%d" % lo)
        passes(accs, spans[0:4], range(4))
        epilogue(accs, spans[0:4])
        store(0, 2048)
        passes(accs, spans[4:6], range(4))
        epilogue(accs, spans[4:6])
        store(2048, 3072)
        passes(accs, spans[6:7], range(4))
        epilogue(accs, spans[6:7])
        store(3072, 3584)
        passes(accs, spans[7:9], range(4))
        epilogue(accs, spans[7:9])
        store(3584, 3840)
        store(3840, 4096)
